import numpy as np
import ml_dtypes


def mxq(x, axis, fmt="e4m3"):
    dtype, down = {"e4m3": (ml_dtypes.float8_e4m3fn, 7), "e5m2": (ml_dtypes.float8_e5m2, 14)}[fmt]
    v = np.moveaxis(np.asarray(x, np.float32).astype(ml_dtypes.bfloat16).astype(np.float64), axis, -1)
    blocks = v.reshape(v.shape[:-1] + (-1, 32))
    amax = np.abs(blocks).max(-1, keepdims=True)
    byte = np.maximum(np.where(amax > 0, np.frexp(amax)[1] - 1 + 127, 0) - down, 1)
    scale = np.exp2(byte - 127.0)
    codes = (blocks / scale).astype(np.float32).astype(dtype).astype(np.float64)
    return np.moveaxis((codes * scale).reshape(v.shape), -1, axis)


WIDE = False


def mx_kscale(k):
    if not WIDE:
        return np.ones(k)
    levels = np.array([10, -10, 5, -5, 0])
    a = np.random.permutation(np.resize(levels, k // 512 * 4)).reshape(k // 512, 4)
    idx = np.arange(k)
    return np.exp2(a[idx // 512, idx % 128 // 32])


BF16 = ml_dtypes.bfloat16


def bf(x):
    return np.asarray(x, np.float32).astype(BF16)


def f64(x):
    return np.asarray(x).astype(np.float64)


B, N1, N2, D, H, FF = 2, 128, 256, 1024, 16, 4096
T = B * (N1 + N2)
EPS = 1e-5


def layer_norm(x, g, b):
    m = x.mean(-1, keepdims=True)
    v = ((x - m) * (x - m)).mean(-1, keepdims=True)
    return (x - m) * (1.0 / np.sqrt(v + EPS)) * g + b


def erf(z):
    a = np.minimum(np.abs(z), 6.0)
    a2 = a * a
    term, tot, n = a.copy(), a.copy(), 1.5
    while np.any(term > 1e-17 * tot):
        term = term * a2 / n
        tot = tot + term
        n += 1.0
    return np.sign(z) * tot * np.exp(-a2) / np.sqrt(0.25 * np.pi)


def gelu_erf(v):
    return 0.5 * v * (1.0 + erf(v * np.sqrt(0.5)))


def setup_inputs():
    s, t = mx_kscale(D), mx_kscale(D)
    return {"h_attn": bf(0.5 * np.random.standard_normal((T, D)) * s),
            "x": bf(np.random.standard_normal((T, D))),
            "w_proj": bf(np.random.standard_normal((D, D)) * 1.8 / np.sqrt(D) / s[:, None]),
            "b_proj": bf(0.1 * np.random.standard_normal(D)),
            "ls1": bf(0.6 + 0.2 * np.random.standard_normal(D)),
            "ln2_g": bf((1.0 + 0.1 * np.random.standard_normal(D)) * t),
            "ln2_b": bf(0.1 * np.random.standard_normal(D) * t),
            "w_fc1": bf(np.random.standard_normal((D, FF)) / np.sqrt(D) / t[:, None]),
            "b_fc1": bf(0.1 * np.random.standard_normal(FF))}


def reference(h_attn, x, w_proj, b_proj, ls1, ln2_g, ln2_b, w_fc1, b_fc1):
    p = (mxq(f64(h_attn), 1, "e4m3") @ mxq(f64(w_proj), 0, "e4m3")) + f64(b_proj)
    x_mid = f64(x) + f64(ls1) * p
    h2 = layer_norm(x_mid, f64(ln2_g), f64(ln2_b))
    u = (mxq(h2, 1, "e4m3") @ mxq(f64(w_fc1), 0, "e4m3")) + f64(b_fc1)
    return x_mid, gelu_erf(u)

@@ -1,0 +1,336 @@
+from contextlib import ExitStack
+
+import concourse.mybir as mybir
+from concourse.masks import make_identity
+
+F32 = mybir.dt.float32
+BF16 = mybir.dt.bfloat16
+U32 = mybir.dt.uint32
+U8 = mybir.dt.uint8
+FP8X4 = mybir.dt.float8_e4m3fn_x4
+ACT = mybir.ActivationFunctionType
+ALU = mybir.AluOpType
+
+P = 128
+PACK = 4
+K_PASS = P * PACK
+T, D, FF = 768, 1024, 4096
+PASSES = D // K_PASS
+TOK_TILES = T // P
+D_CHUNKS = D // P
+BANK = 512
+FF_CHUNK = 2 * BANK
+FF_CHUNKS = FF // FF_CHUNK
+TOKEN_GROUPS = ((0, 4), (4, 2))
+EPS = 1e-5
+FLOPS = 2 * T * D * (D + FF)
+
+B_PROJ, LS1, LN_G, LN_B = 0, D_CHUNKS, 2 * D_CHUNKS, 3 * D_CHUNKS
+
+
+def quantise_weight_unit(nc, stage, unit, rows, codes, scales):
+    grouped = stage.tile([P, BANK * PACK], BF16, tag="grouped", align_bytes=64)
+    dst = grouped[:].rearrange("p (c i t) -> p c t i", i=4, t=PACK)
+    src = rows.rearrange("p t (c i) -> p c t i", i=4)
+    if unit % 2 == 0:
+        nc.vector.tensor_copy(out=dst, in_=src)
+    else:
+        nc.scalar.copy(out=dst, in_=src)
+    nc.vector.quantize_mx(out=codes.bitcast(FP8X4), scales=scales, in_=grouped[:])
+
+
+def tile_nestedtensorblock_pb_kernel(
+    tc, h_attn, x, w_proj, b_proj, ls1, ln2_g, ln2_b, w_fc1, b_fc1, out_0, out_1
+):
+    nc = tc.nc
+    with ExitStack() as ctx:
+        const = ctx.enter_context(tc.tile_pool(name="const", bufs=1))
+        tokens = ctx.enter_context(tc.tile_pool(name="tokens", bufs=1))
+        weights = ctx.enter_context(tc.tile_pool(name="weights", bufs=1))
+        stage = ctx.enter_context(tc.tile_pool(name="stage", bufs=4))
+        work = ctx.enter_context(tc.tile_pool(name="work", bufs=8))
+        psum = ctx.enter_context(tc.psum_pool(name="psum", bufs=2))
+
+        h_rows = tokens.tile([P, TOK_TILES * D], BF16, tag="tok_rows")
+        h_view = h_attn.rearrange("(m p) d -> p m d", p=P)
+
+        def load_h(pair):
+            nc.sync.dma_start(
+                out=h_rows[:, 2 * D * pair : 2 * D * (pair + 1)].rearrange(
+                    "p (m d) -> p m d", m=2
+                ),
+                in_=h_view[:, 2 * pair : 2 * pair + 2, :],
+            )
+
+        wp_rows = weights.tile([P, PASSES, PACK, D], BF16, tag="w_rows", bufs=4)
+        wp_view = w_proj.rearrange("(g u q e) n -> q g u e n", g=PASSES, u=2, e=2)
+
+        def load_wp(g):
+            for u in range(2):
+                nc.sync.dma_start(
+                    out=wp_rows[:, g, 2 * u : 2 * u + 2, :], in_=wp_view[:, g, u, :, :]
+                )
+
+        wf_view = w_fc1.rearrange("(g t p) n -> p g t n", g=PASSES, t=PACK)
+
+        def load_wf(n):
+            rows = weights.tile(
+                [P, PASSES, PACK, FF_CHUNK], BF16, tag="w_rows", bufs=4, name="wf_rows%d" % n
+            )
+            for g in range(PASSES):
+                nc.sync.dma_start(
+                    out=rows[:, g, :, :],
+                    in_=wf_view[:, g, :, FF_CHUNK * n : FF_CHUNK * (n + 1)],
+                )
+            return rows
+
+        load_h(0)
+        load_wp(0)
+        load_h(1)
+        load_h(2)
+        load_wp(1)
+        x_rows = const.tile([P, TOK_TILES, D], BF16)
+        nc.sync.dma_start(out=x_rows[:], in_=x.rearrange("(m p) d -> p m d", p=P))
+        wf_rows = [load_wf(0)]
+        bias_fc1 = const.tile([P, FF], BF16)
+        nc.sync.dma_start(out=bias_fc1[:], in_=b_fc1.partition_broadcast(P))
+        wf_rows.append(load_wf(1))
+        wf_rows.append(load_wf(2))
+
+        ident_f32 = const.tile([P, P], F32)
+        make_identity(nc, ident_f32[:])
+        ident_bf16 = const.tile([P, P], BF16)
+        nc.vector.tensor_copy(out=ident_bf16[:], in_=ident_f32[:])
+        eps = const.tile([P, 1], F32)
+        nc.vector.memset(eps[:], EPS)
+        first_sqrt = const.tile([P, 1], F32)
+        nc.scalar.activation(out=first_sqrt[:], in_=eps[:], func=ACT.Sqrt)
+
+        vec_rows = const.tile([P, P], BF16)
+        nc.vector.memset(vec_rows[:], 0.0)
+        for first_row, vec in ((B_PROJ, b_proj), (LS1, ls1), (LN_G, ln2_g), (LN_B, ln2_b)):
+            nc.scalar.dma_start(
+                out=vec_rows[first_row : first_row + D_CHUNKS, :],
+                in_=vec.rearrange("(r c) -> r c", c=P),
+            )
+        vec_ps = psum.tile([P, P], BF16, tag="turn", bufs=3)
+        nc.tensor.transpose(vec_ps[:], vec_rows[:], ident_bf16[:])
+        vec_cols = const.tile([P, 4 * D_CHUNKS], F32)
+        nc.vector.tensor_copy(out=vec_cols[:], in_=vec_ps[:, 0 : 4 * D_CHUNKS])
+        ls1_b = const.tile([P, D_CHUNKS], F32)
+        nc.vector.tensor_mul(
+            ls1_b[:], vec_cols[:, LS1 : LS1 + D_CHUNKS], vec_cols[:, B_PROJ : B_PROJ + D_CHUNKS]
+        )
+
+        h_words = h_rows[:].bitcast(F32)
+        h_grouped = tokens.tile([P, PASSES * T * PACK], BF16, tag="tok_grouped", align_bytes=64)
+        h_grouped_words = h_grouped[:].bitcast(F32).rearrange(
+            "p (g r u) -> p g r u", g=PASSES, u=2
+        )
+        h_codes = tokens.tile([P, PASSES * T], U32, tag="tok_codes", align_bytes=64)
+        h_scales = tokens.tile([P, PASSES * T], U8, tag="tok_scales", align_bytes=64)
+        for pair in range(TOK_TILES // 2):
+            for m in (2 * pair, 2 * pair + 1):
+                turned = psum.tile([P, PASSES, 2, P], F32, tag="turn", bufs=3)
+                for g in range(PASSES):
+                    for u in range(2):
+                        first_word = (D // 2) * m + (K_PASS // 2) * g + P * u
+                        nc.tensor.transpose(
+                            turned[:, g, u, :],
+                            h_words[:, first_word : first_word + P],
+                            ident_f32[:],
+                        )
+                nc.vector.tensor_copy(
+                    out=h_grouped_words[:, :, P * m : P * (m + 1), :],
+                    in_=turned[:].rearrange("p g u r -> p g r u"),
+                )
+            for g in range(PASSES):
+                first = T * g + 2 * P * pair
+                nc.vector.quantize_mx(
+                    out=h_codes[:, first : first + 2 * P].bitcast(FP8X4),
+                    scales=h_scales[:, first : first + 2 * P],
+                    in_=h_grouped[:, PACK * first : PACK * (first + 2 * P)],
+                )
+
+        wp_codes = weights.tile([P, PASSES * D], U32, align_bytes=64)
+        wp_scales = weights.tile([P, PASSES * D], U8, align_bytes=64)
+        unit = 0
+        for g in range(PASSES):
+            for half in range(D // BANK):
+                first = D * g + BANK * half
+                quantise_weight_unit(
+                    nc,
+                    stage,
+                    unit,
+                    wp_rows[:, g, :, BANK * half : BANK * (half + 1)],
+                    wp_codes[:, first : first + BANK],
+                    wp_scales[:, first : first + BANK],
+                )
+                unit += 1
+        wf_rows.append(load_wf(3))
+
+        x_mid = const.tile([P, TOK_TILES, D], F32)
+        half_sums = const.tile([P, TOK_TILES, 2], F32)
+        neg_mean = const.tile([P, TOK_TILES], F32)
+        sum_sq = const.tile([P, TOK_TILES], F32)
+        for half in range(2):
+            branch_t = []
+            for c in range(4 * half, 4 * half + 4):
+                scaled = work.tile([P, T], F32, tag="f32", name="branch_t%d" % c)
+                for m0, count in TOKEN_GROUPS:
+                    acc = psum.tile([P, BANK], F32, tag="acc1", bufs=2)
+                    for g in range(PASSES):
+                        w_first = D * g + P * c
+                        t_first = T * g + P * m0
+                        nc.tensor.matmul_mx(
+                            out=acc[:, 0 : P * count],
+                            lhsT=wp_codes[:, w_first : w_first + P].bitcast(FP8X4),
+                            lhsT_scale=wp_scales[:, w_first : w_first + P],
+                            rhs=h_codes[:, t_first : t_first + P * count].bitcast(FP8X4),
+                            rhs_scale=h_scales[:, t_first : t_first + P * count],
+                            start=(g == 0),
+                            stop=(g == PASSES - 1),
+                        )
+                    nc.scalar.activation(
+                        out=scaled[:, P * m0 : P * (m0 + count)],
+                        in_=acc[:, 0 : P * count],
+                        func=ACT.Identity,
+                        scale=vec_cols[:, LS1 + c : LS1 + c + 1],
+                        bias=ls1_b[:, c : c + 1],
+                    )
+                branch_t.append(scaled)
+            for m in range(TOK_TILES):
+                branch = psum.tile([P, BANK], F32, tag="turn", bufs=3)
+                for q in range(4):
+                    nc.tensor.transpose(
+                        branch[:, P * q : P * (q + 1)],
+                        branch_t[q][:, P * m : P * (m + 1)],
+                        ident_f32[:],
+                    )
+                nc.vector.scalar_tensor_tensor(
+                    out=x_mid[:, m, BANK * half : BANK * (half + 1)],
+                    in0=branch[:],
+                    scalar=1.0,
+                    in1=x_rows[:, m, BANK * half : BANK * (half + 1)],
+                    op0=ALU.mult,
+                    op1=ALU.add,
+                    accum_out=half_sums[:, m, half : half + 1],
+                )
+
+        x_hat = []
+        for m in range(TOK_TILES):
+            nc.sync.dma_start(out=out_0[P * m : P * (m + 1), :], in_=x_mid[:, m, :])
+            nc.vector.tensor_scalar(
+                out=neg_mean[:, m : m + 1],
+                in0=half_sums[:, m, 0:1],
+                scalar1=half_sums[:, m, 1:2],
+                scalar2=-1.0 / D,
+                op0=ALU.add,
+                op1=ALU.mult,
+            )
+            normed = work.tile([P, D], F32, tag="f32", name="x_hat%d" % m)
+            nc.scalar.activation(
+                out=normed[:],
+                in_=x_mid[:, m, :],
+                func=ACT.Square,
+                bias=neg_mean[:, m : m + 1],
+                scale=1.0,
+                accum_out=sum_sq[:, m : m + 1],
+            )
+            x_hat.append(normed)
+        std = const.tile([P, TOK_TILES], F32)
+        nc.scalar.activation(out=std[:], in_=sum_sq[:], func=ACT.Sqrt, scale=1.0 / D, bias=eps[:])
+        rstd = const.tile([P, TOK_TILES], F32)
+        nc.vector.reciprocal(out=rstd[:], in_=std[:])
+        for m in range(TOK_TILES):
+            nc.vector.tensor_scalar(
+                out=x_hat[m][:],
+                in0=x_mid[:, m, :],
+                scalar1=neg_mean[:, m : m + 1],
+                scalar2=rstd[:, m : m + 1],
+                op0=ALU.add,
+                op1=ALU.mult,
+            )
+
+        h2_planes = tokens.tile([P, D_CHUNKS * T], BF16, tag="tok_rows")
+        h2_grouped = tokens.tile([P, PASSES * T * PACK], BF16, tag="tok_grouped", align_bytes=64)
+        h2_codes = tokens.tile([P, PASSES * T], U32, tag="tok_codes", align_bytes=64)
+        h2_scales = tokens.tile([P, PASSES * T], U8, tag="tok_scales", align_bytes=64)
+        h2_chunks = h2_planes[:].rearrange("p (c r) -> p c r", c=D_CHUNKS)
+        for m0, count in TOKEN_GROUPS:
+            for c in range(D_CHUNKS):
+                turned = psum.tile([P, BANK], F32, tag="turn", bufs=3)
+                for i in range(count):
+                    nc.tensor.transpose(
+                        turned[:, P * i : P * (i + 1)],
+                        x_hat[m0 + i][:, P * c : P * (c + 1)],
+                        ident_f32[:],
+                    )
+                nc.scalar.activation(
+                    out=h2_chunks[:, c, P * m0 : P * (m0 + count)],
+                    in_=turned[:, 0 : P * count],
+                    func=ACT.Identity,
+                    scale=vec_cols[:, LN_G + c : LN_G + c + 1],
+                    bias=vec_cols[:, LN_B + c : LN_B + c + 1],
+                )
+            for g in range(PASSES):
+                first = T * g + P * m0
+                nc.vector.tensor_copy(
+                    out=h2_grouped[:, PACK * first : PACK * (first + P * count)].rearrange(
+                        "p (c i t) -> p c t i", i=4, t=PACK
+                    ),
+                    in_=h2_chunks[:, PACK * g : PACK * (g + 1), P * m0 : P * (m0 + count)].rearrange(
+                        "p t (c i) -> p c t i", i=4
+                    ),
+                )
+            for g in range(PASSES):
+                first = T * g + P * m0
+                nc.vector.quantize_mx(
+                    out=h2_codes[:, first : first + P * count].bitcast(FP8X4),
+                    scales=h2_scales[:, first : first + P * count],
+                    in_=h2_grouped[:, PACK * first : PACK * (first + P * count)],
+                )
+
+        for n in range(FF_CHUNKS):
+            wf_codes = weights.tile([P, PASSES * FF_CHUNK], U32, bufs=3, align_bytes=64)
+            wf_scales = weights.tile([P, PASSES * FF_CHUNK], U8, bufs=3, align_bytes=64)
+            for half in range(FF_CHUNK // BANK):
+                for g in range(PASSES):
+                    first = FF_CHUNK * g + BANK * half
+                    quantise_weight_unit(
+                        nc,
+                        stage,
+                        unit,
+                        wf_rows[n][:, g, :, BANK * half : BANK * (half + 1)],
+                        wf_codes[:, first : first + BANK],
+                        wf_scales[:, first : first + BANK],
+                    )
+                    unit += 1
+            for m in range(TOK_TILES):
+                hidden = work.tile([P, FF_CHUNK], F32, tag="f32")
+                for half in range(FF_CHUNK // BANK):
+                    acc = psum.tile([P, BANK], F32, tag="acc2", bufs=3)
+                    for g in range(PASSES):
+                        t_first = T * g + P * m
+                        w_first = FF_CHUNK * g + BANK * half
+                        nc.tensor.matmul_mx(
+                            out=acc[:],
+                            lhsT=h2_codes[:, t_first : t_first + P].bitcast(FP8X4),
+                            lhsT_scale=h2_scales[:, t_first : t_first + P],
+                            rhs=wf_codes[:, w_first : w_first + BANK].bitcast(FP8X4),
+                            rhs_scale=wf_scales[:, w_first : w_first + BANK],
+                            start=(g == 0),
+                            stop=(g == PASSES - 1),
+                        )
+                    ff_first = FF_CHUNK * n + BANK * half
+                    nc.vector.tensor_tensor(
+                        out=hidden[:, BANK * half : BANK * (half + 1)],
+                        in0=acc[:],
+                        in1=bias_fc1[:, ff_first : ff_first + BANK],
+                        op=ALU.add,
+                    )
+                nc.scalar.activation(out=hidden[:], in_=hidden[:], func=ACT.Gelu)
+                nc.sync.dma_start(
+                    out=out_1[P * m : P * (m + 1), FF_CHUNK * n : FF_CHUNK * (n + 1)],
+                    in_=hidden[:],
+                )

@@ -19,24 +19,15 @@ PASSES = D // K_PASS
 TOK_TILES = T // P
 D_CHUNKS = D // P
 BANK = 512
-FF_CHUNK = 2 * BANK
-FF_CHUNKS = FF // FF_CHUNK
+BLOCK = 2 * BANK
+FF_BLOCKS = FF // BLOCK
+UNITS_PER_BLOCK = PASSES * (BLOCK // BANK)
 TOKEN_GROUPS = ((0, 4), (4, 2))
+FIRST_UNIT_LEFT = 2 * UNITS_PER_BLOCK
 EPS = 1e-5
 FLOPS = 2 * T * D * (D + FF)
 
 B_PROJ, LS1, LN_G, LN_B = 0, D_CHUNKS, 2 * D_CHUNKS, 3 * D_CHUNKS
-
-
-def quantise_weight_unit(nc, stage, unit, rows, codes, scales):
-    grouped = stage.tile([P, BANK * PACK], BF16, tag="grouped", align_bytes=64)
-    dst = grouped[:].rearrange("p (c i t) -> p c t i", i=4, t=PACK)
-    src = rows.rearrange("p t (c i) -> p c t i", i=4)
-    if unit % 2 == 0:
-        nc.vector.tensor_copy(out=dst, in_=src)
-    else:
-        nc.scalar.copy(out=dst, in_=src)
-    nc.vector.quantize_mx(out=codes.bitcast(FP8X4), scales=scales, in_=grouped[:])
 
 
 def tile_nestedtensorblock_pb_kernel(
@@ -44,67 +35,13 @@ def tile_nestedtensorblock_pb_kernel(
 ):
     nc = tc.nc
     with ExitStack() as ctx:
+        ctx.enter_context(tc.manual_schedule())
         const = ctx.enter_context(tc.tile_pool(name="const", bufs=1))
         tokens = ctx.enter_context(tc.tile_pool(name="tokens", bufs=1))
-        weights = ctx.enter_context(tc.tile_pool(name="weights", bufs=1))
+        weights = ctx.enter_context(tc.tile_pool(name="weights", bufs=4))
         stage = ctx.enter_context(tc.tile_pool(name="stage", bufs=4))
         work = ctx.enter_context(tc.tile_pool(name="work", bufs=8))
-        psum = ctx.enter_context(tc.psum_pool(name="psum", bufs=2))
-
-        h_rows = tokens.tile([P, TOK_TILES * D], BF16, tag="tok_rows")
-        h_view = h_attn.rearrange("(m p) d -> p m d", p=P)
-
-        def load_h(pair):
-            nc.sync.dma_start(
-                out=h_rows[:, 2 * D * pair : 2 * D * (pair + 1)].rearrange(
-                    "p (m d) -> p m d", m=2
-                ),
-                in_=h_view[:, 2 * pair : 2 * pair + 2, :],
-            )
-
-        wp_rows = weights.tile([P, PASSES, PACK, D], BF16, tag="w_rows", bufs=4)
-        wp_view = w_proj.rearrange("(g u q e) n -> q g u e n", g=PASSES, u=2, e=2)
-
-        def load_wp(g):
-            for u in range(2):
-                nc.sync.dma_start(
-                    out=wp_rows[:, g, 2 * u : 2 * u + 2, :], in_=wp_view[:, g, u, :, :]
-                )
-
-        wf_view = w_fc1.rearrange("(g t p) n -> p g t n", g=PASSES, t=PACK)
-
-        def load_wf(n):
-            rows = weights.tile(
-                [P, PASSES, PACK, FF_CHUNK], BF16, tag="w_rows", bufs=4, name="wf_rows%d" % n
-            )
-            for g in range(PASSES):
-                nc.sync.dma_start(
-                    out=rows[:, g, :, :],
-                    in_=wf_view[:, g, :, FF_CHUNK * n : FF_CHUNK * (n + 1)],
-                )
-            return rows
-
-        load_h(0)
-        load_wp(0)
-        load_h(1)
-        load_h(2)
-        load_wp(1)
-        x_rows = const.tile([P, TOK_TILES, D], BF16)
-        nc.sync.dma_start(out=x_rows[:], in_=x.rearrange("(m p) d -> p m d", p=P))
-        wf_rows = [load_wf(0)]
-        bias_fc1 = const.tile([P, FF], BF16)
-        nc.sync.dma_start(out=bias_fc1[:], in_=b_fc1.partition_broadcast(P))
-        wf_rows.append(load_wf(1))
-        wf_rows.append(load_wf(2))
-
-        ident_f32 = const.tile([P, P], F32)
-        make_identity(nc, ident_f32[:])
-        ident_bf16 = const.tile([P, P], BF16)
-        nc.vector.tensor_copy(out=ident_bf16[:], in_=ident_f32[:])
-        eps = const.tile([P, 1], F32)
-        nc.vector.memset(eps[:], EPS)
-        first_sqrt = const.tile([P, 1], F32)
-        nc.scalar.activation(out=first_sqrt[:], in_=eps[:], func=ACT.Sqrt)
+        psum = ctx.enter_context(tc.psum_pool(name="psum", bufs=1))
 
         vec_rows = const.tile([P, P], BF16)
         nc.vector.memset(vec_rows[:], 0.0)
@@ -113,6 +50,113 @@ def tile_nestedtensorblock_pb_kernel(
                 out=vec_rows[first_row : first_row + D_CHUNKS, :],
                 in_=vec.rearrange("(r c) -> r c", c=P),
             )
+        bias_row = tokens.tile([P, FF], BF16, tag="tok_b", align_bytes=64)
+        nc.vector.memset(bias_row[:], 0.0)
+        nc.scalar.dma_start(out=bias_row[0:1, :], in_=b_fc1.rearrange("(o n) -> o n", o=1))
+
+        block_rows = {}
+        block_codes = {}
+        block_scales = {}
+
+        def new_block_rows(b):
+            block_rows[b] = weights.tile(
+                [P, PASSES, PACK, BLOCK], BF16, tag="w_rows", name="w_rows%d" % b
+            )
+
+        def new_block_codes(b):
+            block_codes[b] = weights.tile(
+                [P, PASSES * BLOCK], U32, tag="w_codes", name="w_codes%d" % b, align_bytes=64
+            )
+            block_scales[b] = weights.tile(
+                [P, PASSES * BLOCK], U8, tag="w_scales", name="w_scales%d" % b, align_bytes=64
+            )
+
+        new_block_rows(0)
+        wp_view = w_proj.rearrange("(g u q e) n -> q g u e n", g=PASSES, u=2, e=2)
+        for g in range(PASSES):
+            for u in range(2):
+                nc.sync.dma_start(
+                    out=block_rows[0][:, g, 2 * u : 2 * u + 2, :], in_=wp_view[:, g, u, :, :]
+                )
+
+        h_rows = tokens.tile([P, TOK_TILES * D], BF16, tag="tok_a")
+        h_view = h_attn.rearrange("(p m) d -> p m d", p=P)
+        for pair in range(TOK_TILES // 2):
+            nc.sync.dma_start(
+                out=h_rows[:, 2 * D * pair : 2 * D * (pair + 1)].rearrange("p (m d) -> p m d", m=2),
+                in_=h_view[:, 2 * pair : 2 * pair + 2, :],
+            )
+
+        wf_view = w_fc1.rearrange("(g t p) n -> p g t n", g=PASSES, t=PACK)
+
+        def load_ff_block(b):
+            new_block_rows(b)
+            for g in range(PASSES):
+                nc.sync.dma_start(
+                    out=block_rows[b][:, g, :, :],
+                    in_=wf_view[:, g, :, BLOCK * (b - 1) : BLOCK * b],
+                )
+
+        load_ff_block(1)
+        x_rows = const.tile([P, TOK_TILES, D], BF16)
+        nc.sync.dma_start(out=x_rows[:], in_=x.rearrange("(p m) d -> p m d", p=P))
+        load_ff_block(2)
+        load_ff_block(3)
+
+        ident_f32 = const.tile([P, P], F32)
+        make_identity(nc, ident_f32[:])
+        ident_bf16 = const.tile([P, P], BF16)
+        nc.vector.tensor_copy(out=ident_bf16[:], in_=ident_f32[:])
+        neg_half = const.tile([P, 1], F32)
+        nc.vector.memset(neg_half[:], -0.5)
+        first_gelu = const.tile([P, 1], F32)
+        nc.scalar.activation(out=first_gelu[:], in_=neg_half[:], func=ACT.Gelu)
+
+        ones = const.tile([P, P], BF16)
+        nc.vector.memset(ones[:], 1.0)
+        bias_fc1 = const.tile([P, FF], BF16)
+        for b in range(FF_BLOCKS):
+            repeated = psum.tile([P, BLOCK], BF16, tag="acc", bufs=5)
+            for half in range(BLOCK // BANK):
+                first = BLOCK * b + BANK * half
+                nc.tensor.matmul(
+                    out=repeated[:, BANK * half : BANK * (half + 1)],
+                    lhsT=ones[:],
+                    rhs=bias_row[:, first : first + BANK],
+                    start=True,
+                    stop=True,
+                )
+            copy_out = nc.scalar.copy if b % 2 == 0 else nc.vector.tensor_copy
+            copy_out(out=bias_fc1[:, BLOCK * b : BLOCK * (b + 1)], in_=repeated[:])
+
+        for b in range(4):
+            new_block_codes(b)
+        grouped_units = {}
+
+        def regroup_unit(u, copy):
+            b, g, half = u // UNITS_PER_BLOCK, (u % UNITS_PER_BLOCK) // 2, u % 2
+            grouped = stage.tile(
+                [P, BANK * PACK], BF16, tag="grouped", name="grouped%d" % u, align_bytes=64
+            )
+            copy(
+                out=grouped[:].rearrange("p (c i t) -> p c t i", i=4, t=PACK),
+                in_=block_rows[b][:, g, :, BANK * half : BANK * (half + 1)].rearrange(
+                    "p t (c i) -> p c t i", i=4
+                ),
+            )
+            grouped_units[u] = grouped
+
+        def quantise_unit(u):
+            b, g, half = u // UNITS_PER_BLOCK, (u % UNITS_PER_BLOCK) // 2, u % 2
+            first = BLOCK * g + BANK * half
+            nc.vector.quantize_mx(
+                out=block_codes[b][:, first : first + BANK].bitcast(FP8X4),
+                scales=block_scales[b][:, first : first + BANK],
+                in_=grouped_units[u][:],
+            )
+
+        regroup_unit(0, nc.vector.tensor_copy)
+        regroup_unit(1, nc.scalar.copy)
         vec_ps = psum.tile([P, P], BF16, tag="turn", bufs=3)
         nc.tensor.transpose(vec_ps[:], vec_rows[:], ident_bf16[:])
         vec_cols = const.tile([P, 4 * D_CHUNKS], F32)
@@ -121,9 +165,17 @@ def tile_nestedtensorblock_pb_kernel(
         nc.vector.tensor_mul(
             ls1_b[:], vec_cols[:, LS1 : LS1 + D_CHUNKS], vec_cols[:, B_PROJ : B_PROJ + D_CHUNKS]
         )
+        quantise_unit(0)
+        regroup_unit(2, nc.vector.tensor_copy)
+        regroup_unit(3, nc.scalar.copy)
+        quantise_unit(1)
+        quantise_unit(2)
+        quantise_unit(3)
+        load_ff_block(4)
+
 
         h_words = h_rows[:].bitcast(F32)
-        h_grouped = tokens.tile([P, PASSES * T * PACK], BF16, tag="tok_grouped", align_bytes=64)
+        h_grouped = tokens.tile([P, PASSES * T * PACK], BF16, tag="tok_b", align_bytes=64)
         h_grouped_words = h_grouped[:].bitcast(F32).rearrange(
             "p (g r u) -> p g r u", g=PASSES, u=2
         )
@@ -140,7 +192,7 @@ def tile_nestedtensorblock_pb_kernel(
                             h_words[:, first_word : first_word + P],
                             ident_f32[:],
                         )
-                nc.vector.tensor_copy(
+                nc.scalar.copy(
                     out=h_grouped_words[:, :, P * m : P * (m + 1), :],
                     in_=turned[:].rearrange("p g u r -> p g r u"),
                 )
@@ -152,108 +204,117 @@ def tile_nestedtensorblock_pb_kernel(
                     in_=h_grouped[:, PACK * first : PACK * (first + 2 * P)],
                 )
 
-        wp_codes = weights.tile([P, PASSES * D], U32, align_bytes=64)
-        wp_scales = weights.tile([P, PASSES * D], U8, align_bytes=64)
-        unit = 0
-        for g in range(PASSES):
-            for half in range(D // BANK):
-                first = D * g + BANK * half
-                quantise_weight_unit(
-                    nc,
-                    stage,
-                    unit,
-                    wp_rows[:, g, :, BANK * half : BANK * (half + 1)],
-                    wp_codes[:, first : first + BANK],
-                    wp_scales[:, first : first + BANK],
+        branch_t = [
+            tokens.tile([P, 4, T], F32, tag="tok_a", name="branch_t0"),
+            tokens.tile([P, 4, T], F32, tag="tok_b", name="branch_t1", align_bytes=64),
+        ]
+        for c in range(D_CHUNKS):
+            for m0, count in TOKEN_GROUPS:
+                acc = psum.tile([P, BANK], F32, tag="acc", bufs=5)
+                for g in range(PASSES):
+                    w_first = BLOCK * g + P * c
+                    t_first = T * g + P * m0
+                    nc.tensor.matmul_mx(
+                        out=acc[:, 0 : P * count],
+                        lhsT=block_codes[0][:, w_first : w_first + P].bitcast(FP8X4),
+                        lhsT_scale=block_scales[0][:, w_first : w_first + P],
+                        rhs=h_codes[:, t_first : t_first + P * count].bitcast(FP8X4),
+                        rhs_scale=h_scales[:, t_first : t_first + P * count],
+                        start=(g == 0),
+                        stop=(g == PASSES - 1),
+                    )
+                nc.scalar.activation(
+                    out=branch_t[c // 4][:, c % 4, P * m0 : P * (m0 + count)],
+                    in_=acc[:, 0 : P * count],
+                    func=ACT.Identity,
+                    scale=vec_cols[:, LS1 + c : LS1 + c + 1],
+                    bias=ls1_b[:, c : c + 1],
                 )
-                unit += 1
-        wf_rows.append(load_wf(3))
+        new_block_codes(4)
+        regroup_unit(4, nc.vector.tensor_copy)
+        regroup_unit(5, nc.vector.tensor_copy)
+        quantise_unit(4)
+        regroup_unit(6, nc.vector.tensor_copy)
+        quantise_unit(5)
+        regroup_unit(7, nc.vector.tensor_copy)
+        quantise_unit(6)
+        quantise_unit(7)
 
         x_mid = const.tile([P, TOK_TILES, D], F32)
         half_sums = const.tile([P, TOK_TILES, 2], F32)
         neg_mean = const.tile([P, TOK_TILES], F32)
         sum_sq = const.tile([P, TOK_TILES], F32)
-        for half in range(2):
-            branch_t = []
-            for c in range(4 * half, 4 * half + 4):
-                scaled = work.tile([P, T], F32, tag="f32", name="branch_t%d" % c)
-                for m0, count in TOKEN_GROUPS:
-                    acc = psum.tile([P, BANK], F32, tag="acc1", bufs=2)
-                    for g in range(PASSES):
-                        w_first = D * g + P * c
-                        t_first = T * g + P * m0
-                        nc.tensor.matmul_mx(
-                            out=acc[:, 0 : P * count],
-                            lhsT=wp_codes[:, w_first : w_first + P].bitcast(FP8X4),
-                            lhsT_scale=wp_scales[:, w_first : w_first + P],
-                            rhs=h_codes[:, t_first : t_first + P * count].bitcast(FP8X4),
-                            rhs_scale=h_scales[:, t_first : t_first + P * count],
-                            start=(g == 0),
-                            stop=(g == PASSES - 1),
+        var_eps = const.tile([P, TOK_TILES], F32)
+        rstd = const.tile([P, TOK_TILES], F32)
+        x_mid_view = out_0.rearrange("(p m) d -> p m d", p=P)
+        x_hat = []
+        for step in range(TOK_TILES + 2):
+            if step < TOK_TILES:
+                m = step
+                for half in range(2):
+                    branch = psum.tile([P, BANK], F32, tag="turn", bufs=3)
+                    for q in range(4):
+                        nc.tensor.transpose(
+                            branch[:, P * q : P * (q + 1)],
+                            branch_t[half][:, q, P * m : P * (m + 1)],
+                            ident_f32[:],
                         )
-                    nc.scalar.activation(
-                        out=scaled[:, P * m0 : P * (m0 + count)],
-                        in_=acc[:, 0 : P * count],
-                        func=ACT.Identity,
-                        scale=vec_cols[:, LS1 + c : LS1 + c + 1],
-                        bias=ls1_b[:, c : c + 1],
+                    nc.vector.scalar_tensor_tensor(
+                        out=x_mid[:, m, BANK * half : BANK * (half + 1)],
+                        in0=branch[:],
+                        scalar=1.0,
+                        in1=x_rows[:, m, BANK * half : BANK * (half + 1)],
+                        op0=ALU.mult,
+                        op1=ALU.add,
+                        accum_out=half_sums[:, m, half : half + 1],
                     )
-                branch_t.append(scaled)
-            for m in range(TOK_TILES):
-                branch = psum.tile([P, BANK], F32, tag="turn", bufs=3)
-                for q in range(4):
-                    nc.tensor.transpose(
-                        branch[:, P * q : P * (q + 1)],
-                        branch_t[q][:, P * m : P * (m + 1)],
-                        ident_f32[:],
-                    )
-                nc.vector.scalar_tensor_tensor(
-                    out=x_mid[:, m, BANK * half : BANK * (half + 1)],
-                    in0=branch[:],
-                    scalar=1.0,
-                    in1=x_rows[:, m, BANK * half : BANK * (half + 1)],
+                nc.sync.dma_start(out=x_mid_view[:, m, :], in_=x_mid[:, m, :])
+                nc.vector.tensor_scalar(
+                    out=neg_mean[:, m : m + 1],
+                    in0=half_sums[:, m, 0:1],
+                    scalar1=half_sums[:, m, 1:2],
+                    scalar2=-1.0 / D,
+                    op0=ALU.add,
+                    op1=ALU.mult,
+                )
+                normed = work.tile([P, D], F32, tag="f32", name="x_hat%d" % m)
+                nc.scalar.activation(
+                    out=normed[:],
+                    in_=x_mid[:, m, :],
+                    func=ACT.Square,
+                    bias=neg_mean[:, m : m + 1],
+                    scale=1.0,
+                    accum_out=sum_sq[:, m : m + 1],
+                )
+                x_hat.append(normed)
+                if step % 2 == 1:
+                    regroup_unit(FIRST_UNIT_LEFT + step // 2, nc.scalar.copy)
+            if 1 <= step <= TOK_TILES:
+                m = step - 1
+                nc.vector.tensor_scalar(
+                    out=var_eps[:, m : m + 1],
+                    in0=sum_sq[:, m : m + 1],
+                    scalar1=1.0 / D,
+                    scalar2=EPS,
                     op0=ALU.mult,
                     op1=ALU.add,
-                    accum_out=half_sums[:, m, half : half + 1],
+                )
+                nc.gpsimd.tensor_tensor(
+                    out=rstd[:, m : m + 1], in0=var_eps[:, m : m + 1], in1=neg_half[:], op=ALU.pow
+                )
+            if step >= 2:
+                m = step - 2
+                nc.vector.tensor_scalar(
+                    out=x_hat[m][:],
+                    in0=x_mid[:, m, :],
+                    scalar1=neg_mean[:, m : m + 1],
+                    scalar2=rstd[:, m : m + 1],
+                    op0=ALU.add,
+                    op1=ALU.mult,
                 )
 
-        x_hat = []
-        for m in range(TOK_TILES):
-            nc.sync.dma_start(out=out_0[P * m : P * (m + 1), :], in_=x_mid[:, m, :])
-            nc.vector.tensor_scalar(
-                out=neg_mean[:, m : m + 1],
-                in0=half_sums[:, m, 0:1],
-                scalar1=half_sums[:, m, 1:2],
-                scalar2=-1.0 / D,
-                op0=ALU.add,
-                op1=ALU.mult,
-            )
-            normed = work.tile([P, D], F32, tag="f32", name="x_hat%d" % m)
-            nc.scalar.activation(
-                out=normed[:],
-                in_=x_mid[:, m, :],
-                func=ACT.Square,
-                bias=neg_mean[:, m : m + 1],
-                scale=1.0,
-                accum_out=sum_sq[:, m : m + 1],
-            )
-            x_hat.append(normed)
-        std = const.tile([P, TOK_TILES], F32)
-        nc.scalar.activation(out=std[:], in_=sum_sq[:], func=ACT.Sqrt, scale=1.0 / D, bias=eps[:])
-        rstd = const.tile([P, TOK_TILES], F32)
-        nc.vector.reciprocal(out=rstd[:], in_=std[:])
-        for m in range(TOK_TILES):
-            nc.vector.tensor_scalar(
-                out=x_hat[m][:],
-                in0=x_mid[:, m, :],
-                scalar1=neg_mean[:, m : m + 1],
-                scalar2=rstd[:, m : m + 1],
-                op0=ALU.add,
-                op1=ALU.mult,
-            )
-
-        h2_planes = tokens.tile([P, D_CHUNKS * T], BF16, tag="tok_rows")
-        h2_grouped = tokens.tile([P, PASSES * T * PACK], BF16, tag="tok_grouped", align_bytes=64)
+        h2_planes = tokens.tile([P, D_CHUNKS * T], BF16, tag="tok_a")
+        h2_grouped = tokens.tile([P, PASSES * T * PACK], BF16, tag="tok_b", align_bytes=64)
         h2_codes = tokens.tile([P, PASSES * T], U32, tag="tok_codes", align_bytes=64)
         h2_scales = tokens.tile([P, PASSES * T], U8, tag="tok_scales", align_bytes=64)
         h2_chunks = h2_planes[:].rearrange("p (c r) -> p c r", c=D_CHUNKS)
@@ -266,13 +327,25 @@ def tile_nestedtensorblock_pb_kernel(
                         x_hat[m0 + i][:, P * c : P * (c + 1)],
                         ident_f32[:],
                     )
-                nc.scalar.activation(
-                    out=h2_chunks[:, c, P * m0 : P * (m0 + count)],
-                    in_=turned[:, 0 : P * count],
-                    func=ACT.Identity,
-                    scale=vec_cols[:, LN_G + c : LN_G + c + 1],
-                    bias=vec_cols[:, LN_B + c : LN_B + c + 1],
-                )
+                if m0 == 0 and c % 2 == 1:
+                    nc.vector.tensor_scalar(
+                        out=h2_chunks[:, c, P * m0 : P * (m0 + count)],
+                        in0=turned[:, 0 : P * count],
+                        scalar1=vec_cols[:, LN_G + c : LN_G + c + 1],
+                        scalar2=vec_cols[:, LN_B + c : LN_B + c + 1],
+                        op0=ALU.mult,
+                        op1=ALU.add,
+                    )
+                else:
+                    nc.scalar.activation(
+                        out=h2_chunks[:, c, P * m0 : P * (m0 + count)],
+                        in_=turned[:, 0 : P * count],
+                        func=ACT.Identity,
+                        scale=vec_cols[:, LN_G + c : LN_G + c + 1],
+                        bias=vec_cols[:, LN_B + c : LN_B + c + 1],
+                    )
+
+        def quantise_h2(m0, count):
             for g in range(PASSES):
                 first = T * g + P * m0
                 nc.vector.tensor_copy(
@@ -291,46 +364,46 @@ def tile_nestedtensorblock_pb_kernel(
                     in_=h2_grouped[:, PACK * first : PACK * (first + P * count)],
                 )
 
-        for n in range(FF_CHUNKS):
-            wf_codes = weights.tile([P, PASSES * FF_CHUNK], U32, bufs=3, align_bytes=64)
-            wf_scales = weights.tile([P, PASSES * FF_CHUNK], U8, bufs=3, align_bytes=64)
-            for half in range(FF_CHUNK // BANK):
-                for g in range(PASSES):
-                    first = FF_CHUNK * g + BANK * half
-                    quantise_weight_unit(
-                        nc,
-                        stage,
-                        unit,
-                        wf_rows[n][:, g, :, BANK * half : BANK * (half + 1)],
-                        wf_codes[:, first : first + BANK],
-                        wf_scales[:, first : first + BANK],
-                    )
-                    unit += 1
-            for m in range(TOK_TILES):
-                hidden = work.tile([P, FF_CHUNK], F32, tag="f32")
-                for half in range(FF_CHUNK // BANK):
-                    acc = psum.tile([P, BANK], F32, tag="acc2", bufs=3)
-                    for g in range(PASSES):
-                        t_first = T * g + P * m
-                        w_first = FF_CHUNK * g + BANK * half
-                        nc.tensor.matmul_mx(
-                            out=acc[:],
-                            lhsT=h2_codes[:, t_first : t_first + P].bitcast(FP8X4),
-                            lhsT_scale=h2_scales[:, t_first : t_first + P],
-                            rhs=wf_codes[:, w_first : w_first + BANK].bitcast(FP8X4),
-                            rhs_scale=wf_scales[:, w_first : w_first + BANK],
-                            start=(g == 0),
-                            stop=(g == PASSES - 1),
+        g_view = out_1.rearrange("(p m) f -> p m f", p=P)
+        units = UNITS_PER_BLOCK * (1 + FF_BLOCKS)
+        for b in range(1, 1 + FF_BLOCKS):
+            for m0, count in TOKEN_GROUPS:
+                if b == 1:
+                    quantise_h2(m0, count)
+                for m in range(m0, m0 + count):
+                    step = TOK_TILES * (b - 1) + m
+                    to_quantise = FIRST_UNIT_LEFT + step
+                    to_regroup = to_quantise + 3
+                    hidden = work.tile([P, BLOCK], F32, tag="f32")
+                    for half in range(BLOCK // BANK):
+                        acc = psum.tile([P, BANK], F32, tag="acc", bufs=5)
+                        for g in range(PASSES):
+                            t_first = T * g + P * m
+                            w_first = BLOCK * g + BANK * half
+                            nc.tensor.matmul_mx(
+                                out=acc[:],
+                                lhsT=h2_codes[:, t_first : t_first + P].bitcast(FP8X4),
+                                lhsT_scale=h2_scales[:, t_first : t_first + P],
+                                rhs=block_codes[b][:, w_first : w_first + BANK].bitcast(FP8X4),
+                                rhs_scale=block_scales[b][:, w_first : w_first + BANK],
+                                start=(g == 0),
+                                stop=(g == PASSES - 1),
+                            )
+                        ff_first = BLOCK * (b - 1) + BANK * half
+                        nc.vector.tensor_tensor(
+                            out=hidden[:, BANK * half : BANK * (half + 1)],
+                            in0=acc[:],
+                            in1=bias_fc1[:, ff_first : ff_first + BANK],
+                            op=ALU.add,
                         )
-                    ff_first = FF_CHUNK * n + BANK * half
-                    nc.vector.tensor_tensor(
-                        out=hidden[:, BANK * half : BANK * (half + 1)],
-                        in0=acc[:],
-                        in1=bias_fc1[:, ff_first : ff_first + BANK],
-                        op=ALU.add,
+                    if to_quantise < units:
+                        quantise_unit(to_quantise)
+                    if to_regroup < units:
+                        if to_regroup % 2 == 0:
+                            regroup_unit(to_regroup, nc.vector.tensor_copy)
+                        else:
+                            regroup_unit(to_regroup, nc.scalar.copy)
+                    nc.scalar.activation(out=hidden[:], in_=hidden[:], func=ACT.Gelu)
+                    nc.sync.dma_start(
+                        out=g_view[:, m, BLOCK * (b - 1) : BLOCK * b], in_=hidden[:]
                     )
-                nc.scalar.activation(out=hidden[:], in_=hidden[:], func=ACT.Gelu)
-                nc.sync.dma_start(
-                    out=out_1[P * m : P * (m + 1), FF_CHUNK * n : FF_CHUNK * (n + 1)],
-                    in_=hidden[:],
-                )

@@ -24,6 +24,7 @@ FF_BLOCKS = FF // BLOCK
 UNITS_PER_BLOCK = PASSES * (BLOCK // BANK)
 TOKEN_GROUPS = ((0, 4), (4, 2))
 FIRST_UNIT_LEFT = 2 * UNITS_PER_BLOCK
+NORM_LAG = 2
 EPS = 1e-5
 FLOPS = 2 * T * D * (D + FF)
 
@@ -35,7 +36,6 @@ def tile_nestedtensorblock_pb_kernel(
 ):
     nc = tc.nc
     with ExitStack() as ctx:
-        ctx.enter_context(tc.manual_schedule())
         const = ctx.enter_context(tc.tile_pool(name="const", bufs=1))
         tokens = ctx.enter_context(tc.tile_pool(name="tokens", bufs=1))
         weights = ctx.enter_context(tc.tile_pool(name="weights", bufs=4))
@@ -50,9 +50,6 @@ def tile_nestedtensorblock_pb_kernel(
                 out=vec_rows[first_row : first_row + D_CHUNKS, :],
                 in_=vec.rearrange("(r c) -> r c", c=P),
             )
-        bias_row = tokens.tile([P, FF], BF16, tag="tok_b", align_bytes=64)
-        nc.vector.memset(bias_row[:], 0.0)
-        nc.scalar.dma_start(out=bias_row[0:1, :], in_=b_fc1.rearrange("(o n) -> o n", o=1))
 
         block_rows = {}
         block_codes = {}
@@ -112,22 +109,16 @@ def tile_nestedtensorblock_pb_kernel(
         first_gelu = const.tile([P, 1], F32)
         nc.scalar.activation(out=first_gelu[:], in_=neg_half[:], func=ACT.Gelu)
 
-        ones = const.tile([P, P], BF16)
-        nc.vector.memset(ones[:], 1.0)
-        bias_fc1 = const.tile([P, FF], BF16)
-        for b in range(FF_BLOCKS):
-            repeated = psum.tile([P, BLOCK], BF16, tag="acc", bufs=5)
-            for half in range(BLOCK // BANK):
-                first = BLOCK * b + BANK * half
-                nc.tensor.matmul(
-                    out=repeated[:, BANK * half : BANK * (half + 1)],
-                    lhsT=ones[:],
-                    rhs=bias_row[:, first : first + BANK],
-                    start=True,
-                    stop=True,
-                )
-            copy_out = nc.scalar.copy if b % 2 == 0 else nc.vector.tensor_copy
-            copy_out(out=bias_fc1[:, BLOCK * b : BLOCK * (b + 1)], in_=repeated[:])
+        vec_cols = const.tile([P, 4 * D_CHUNKS], F32)
+        ls1_b = const.tile([P, D_CHUNKS], F32)
+
+        def transpose_vectors():
+            vec_ps = psum.tile([P, P], BF16, tag="turn", bufs=3)
+            nc.tensor.transpose(vec_ps[:], vec_rows[:], ident_bf16[:])
+            nc.vector.tensor_copy(out=vec_cols[:], in_=vec_ps[:, 0 : 4 * D_CHUNKS])
+            nc.vector.tensor_mul(
+                ls1_b[:], vec_cols[:, LS1 : LS1 + D_CHUNKS], vec_cols[:, B_PROJ : B_PROJ + D_CHUNKS]
+            )
 
         for b in range(4):
             new_block_codes(b)
@@ -157,14 +148,6 @@ def tile_nestedtensorblock_pb_kernel(
 
         regroup_unit(0, nc.vector.tensor_copy)
         regroup_unit(1, nc.scalar.copy)
-        vec_ps = psum.tile([P, P], BF16, tag="turn", bufs=3)
-        nc.tensor.transpose(vec_ps[:], vec_rows[:], ident_bf16[:])
-        vec_cols = const.tile([P, 4 * D_CHUNKS], F32)
-        nc.vector.tensor_copy(out=vec_cols[:], in_=vec_ps[:, 0 : 4 * D_CHUNKS])
-        ls1_b = const.tile([P, D_CHUNKS], F32)
-        nc.vector.tensor_mul(
-            ls1_b[:], vec_cols[:, LS1 : LS1 + D_CHUNKS], vec_cols[:, B_PROJ : B_PROJ + D_CHUNKS]
-        )
         quantise_unit(0)
         regroup_unit(2, nc.vector.tensor_copy)
         regroup_unit(3, nc.scalar.copy)
@@ -172,6 +155,8 @@ def tile_nestedtensorblock_pb_kernel(
         quantise_unit(2)
         quantise_unit(3)
         load_ff_block(4)
+        bias_fc1 = const.tile([P, FF], BF16)
+        nc.sync.dma_start(out=bias_fc1[:], in_=b_fc1.partition_broadcast(P))
 
 
         h_words = h_rows[:].bitcast(F32)
@@ -203,13 +188,15 @@ def tile_nestedtensorblock_pb_kernel(
                     scales=h_scales[:, first : first + 2 * P],
                     in_=h_grouped[:, PACK * first : PACK * (first + 2 * P)],
                 )
+            if pair == 0:
+                transpose_vectors()
 
         branch_t = [
             tokens.tile([P, 4, T], F32, tag="tok_a", name="branch_t0"),
             tokens.tile([P, 4, T], F32, tag="tok_b", name="branch_t1", align_bytes=64),
         ]
-        for c in range(D_CHUNKS):
-            for m0, count in TOKEN_GROUPS:
+        for m0, count in TOKEN_GROUPS:
+            for c in range(D_CHUNKS):
                 acc = psum.tile([P, BANK], F32, tag="acc", bufs=5)
                 for g in range(PASSES):
                     w_first = BLOCK * g + P * c
@@ -248,7 +235,7 @@ def tile_nestedtensorblock_pb_kernel(
         rstd = const.tile([P, TOK_TILES], F32)
         x_mid_view = out_0.rearrange("(p m) d -> p m d", p=P)
         x_hat = []
-        for step in range(TOK_TILES + 2):
+        for step in range(TOK_TILES + NORM_LAG):
             if step < TOK_TILES:
                 m = step
                 for half in range(2):
@@ -302,8 +289,8 @@ def tile_nestedtensorblock_pb_kernel(
                 nc.gpsimd.tensor_tensor(
                     out=rstd[:, m : m + 1], in0=var_eps[:, m : m + 1], in1=neg_half[:], op=ALU.pow
                 )
-            if step >= 2:
-                m = step - 2
+            if step >= NORM_LAG:
+                m = step - NORM_LAG
                 nc.vector.tensor_scalar(
                     out=x_hat[m][:],
                     in0=x_mid[:, m, :],

@@ -23,8 +23,8 @@ BLOCK = 2 * BANK
 FF_BLOCKS = FF // BLOCK
 UNITS_PER_BLOCK = PASSES * (BLOCK // BANK)
 TOKEN_GROUPS = ((0, 4), (4, 2))
-FIRST_UNIT_LEFT = 2 * UNITS_PER_BLOCK
-NORM_LAG = 2
+FIRST_GPSIMD_UNIT = 3 * UNITS_PER_BLOCK + 2
+STEPS_PER_GPSIMD_UNIT = 3
 EPS = 1e-5
 FLOPS = 2 * T * D * (D + FF)
 
@@ -135,7 +135,7 @@ def tile_nestedtensorblock_pb_kernel(
                     "p t (c i) -> p c t i", i=4
                 ),
             )
-            grouped_units[u] = grouped
+            grouped_units[u] = grouped[:]
 
         def quantise_unit(u):
             b, g, half = u // UNITS_PER_BLOCK, (u % UNITS_PER_BLOCK) // 2, u % 2
@@ -143,7 +143,7 @@ def tile_nestedtensorblock_pb_kernel(
             nc.vector.quantize_mx(
                 out=block_codes[b][:, first : first + BANK].bitcast(FP8X4),
                 scales=block_scales[b][:, first : first + BANK],
-                in_=grouped_units[u][:],
+                in_=grouped_units[u],
             )
 
         regroup_unit(0, nc.vector.tensor_copy)
@@ -235,70 +235,62 @@ def tile_nestedtensorblock_pb_kernel(
         rstd = const.tile([P, TOK_TILES], F32)
         x_mid_view = out_0.rearrange("(p m) d -> p m d", p=P)
         x_hat = []
-        for step in range(TOK_TILES + NORM_LAG):
-            if step < TOK_TILES:
-                m = step
-                for half in range(2):
-                    branch = psum.tile([P, BANK], F32, tag="turn", bufs=3)
-                    for q in range(4):
-                        nc.tensor.transpose(
-                            branch[:, P * q : P * (q + 1)],
-                            branch_t[half][:, q, P * m : P * (m + 1)],
-                            ident_f32[:],
-                        )
-                    nc.vector.scalar_tensor_tensor(
-                        out=x_mid[:, m, BANK * half : BANK * (half + 1)],
-                        in0=branch[:],
-                        scalar=1.0,
-                        in1=x_rows[:, m, BANK * half : BANK * (half + 1)],
-                        op0=ALU.mult,
-                        op1=ALU.add,
-                        accum_out=half_sums[:, m, half : half + 1],
+        for m in range(TOK_TILES):
+            for half in range(2):
+                branch = psum.tile([P, BANK], F32, tag="turn", bufs=3)
+                for q in range(4):
+                    nc.tensor.transpose(
+                        branch[:, P * q : P * (q + 1)],
+                        branch_t[half][:, q, P * m : P * (m + 1)],
+                        ident_f32[:],
                     )
-                nc.sync.dma_start(out=x_mid_view[:, m, :], in_=x_mid[:, m, :])
-                nc.vector.tensor_scalar(
-                    out=neg_mean[:, m : m + 1],
-                    in0=half_sums[:, m, 0:1],
-                    scalar1=half_sums[:, m, 1:2],
-                    scalar2=-1.0 / D,
-                    op0=ALU.add,
-                    op1=ALU.mult,
-                )
-                normed = work.tile([P, D], F32, tag="f32", name="x_hat%d" % m)
-                nc.scalar.activation(
-                    out=normed[:],
-                    in_=x_mid[:, m, :],
-                    func=ACT.Square,
-                    bias=neg_mean[:, m : m + 1],
-                    scale=1.0,
-                    accum_out=sum_sq[:, m : m + 1],
-                )
-                x_hat.append(normed)
-                if step % 2 == 1:
-                    regroup_unit(FIRST_UNIT_LEFT + step // 2, nc.scalar.copy)
-            if 1 <= step <= TOK_TILES:
-                m = step - 1
-                nc.vector.tensor_scalar(
-                    out=var_eps[:, m : m + 1],
-                    in0=sum_sq[:, m : m + 1],
-                    scalar1=1.0 / D,
-                    scalar2=EPS,
+                nc.vector.scalar_tensor_tensor(
+                    out=x_mid[:, m, BANK * half : BANK * (half + 1)],
+                    in0=branch[:],
+                    scalar=1.0,
+                    in1=x_rows[:, m, BANK * half : BANK * (half + 1)],
                     op0=ALU.mult,
                     op1=ALU.add,
+                    accum_out=half_sums[:, m, half : half + 1],
                 )
-                nc.gpsimd.tensor_tensor(
-                    out=rstd[:, m : m + 1], in0=var_eps[:, m : m + 1], in1=neg_half[:], op=ALU.pow
-                )
-            if step >= NORM_LAG:
-                m = step - NORM_LAG
-                nc.vector.tensor_scalar(
-                    out=x_hat[m][:],
-                    in0=x_mid[:, m, :],
-                    scalar1=neg_mean[:, m : m + 1],
-                    scalar2=rstd[:, m : m + 1],
-                    op0=ALU.add,
-                    op1=ALU.mult,
-                )
+            nc.sync.dma_start(out=x_mid_view[:, m, :], in_=x_mid[:, m, :])
+            nc.vector.tensor_scalar(
+                out=neg_mean[:, m : m + 1],
+                in0=half_sums[:, m, 0:1],
+                scalar1=half_sums[:, m, 1:2],
+                scalar2=-1.0 / D,
+                op0=ALU.add,
+                op1=ALU.mult,
+            )
+            normed = work.tile([P, D], F32, tag="f32", name="x_hat%d" % m)
+            nc.scalar.activation(
+                out=normed[:],
+                in_=x_mid[:, m, :],
+                func=ACT.Square,
+                bias=neg_mean[:, m : m + 1],
+                scale=1.0,
+                accum_out=sum_sq[:, m : m + 1],
+            )
+            nc.vector.tensor_scalar(
+                out=var_eps[:, m : m + 1],
+                in0=sum_sq[:, m : m + 1],
+                scalar1=1.0 / D,
+                scalar2=EPS,
+                op0=ALU.mult,
+                op1=ALU.add,
+            )
+            nc.gpsimd.tensor_tensor(
+                out=rstd[:, m : m + 1], in0=var_eps[:, m : m + 1], in1=neg_half[:], op=ALU.pow
+            )
+            nc.vector.tensor_scalar(
+                out=normed[:],
+                in0=x_mid[:, m, :],
+                scalar1=neg_mean[:, m : m + 1],
+                scalar2=rstd[:, m : m + 1],
+                op0=ALU.add,
+                op1=ALU.mult,
+            )
+            x_hat.append(normed)
 
         h2_planes = tokens.tile([P, D_CHUNKS * T], BF16, tag="tok_a")
         h2_grouped = tokens.tile([P, PASSES * T * PACK], BF16, tag="tok_b", align_bytes=64)
@@ -314,25 +306,13 @@ def tile_nestedtensorblock_pb_kernel(
                         x_hat[m0 + i][:, P * c : P * (c + 1)],
                         ident_f32[:],
                     )
-                if m0 == 0 and c % 2 == 1:
-                    nc.vector.tensor_scalar(
-                        out=h2_chunks[:, c, P * m0 : P * (m0 + count)],
-                        in0=turned[:, 0 : P * count],
-                        scalar1=vec_cols[:, LN_G + c : LN_G + c + 1],
-                        scalar2=vec_cols[:, LN_B + c : LN_B + c + 1],
-                        op0=ALU.mult,
-                        op1=ALU.add,
-                    )
-                else:
-                    nc.scalar.activation(
-                        out=h2_chunks[:, c, P * m0 : P * (m0 + count)],
-                        in_=turned[:, 0 : P * count],
-                        func=ACT.Identity,
-                        scale=vec_cols[:, LN_G + c : LN_G + c + 1],
-                        bias=vec_cols[:, LN_B + c : LN_B + c + 1],
-                    )
-
-        def quantise_h2(m0, count):
+                nc.scalar.activation(
+                    out=h2_chunks[:, c, P * m0 : P * (m0 + count)],
+                    in_=turned[:, 0 : P * count],
+                    func=ACT.Identity,
+                    scale=vec_cols[:, LN_G + c : LN_G + c + 1],
+                    bias=vec_cols[:, LN_B + c : LN_B + c + 1],
+                )
             for g in range(PASSES):
                 first = T * g + P * m0
                 nc.vector.tensor_copy(
@@ -351,46 +331,64 @@ def tile_nestedtensorblock_pb_kernel(
                     in_=h2_grouped[:, PACK * first : PACK * (first + P * count)],
                 )
 
+        for u in range(2 * UNITS_PER_BLOCK, 3 * UNITS_PER_BLOCK):
+            regroup_unit(u, nc.scalar.copy)
+        for u in range(2 * UNITS_PER_BLOCK, 3 * UNITS_PER_BLOCK):
+            quantise_unit(u)
+        for u in range(3 * UNITS_PER_BLOCK, FIRST_GPSIMD_UNIT):
+            regroup_unit(u, nc.vector.tensor_copy)
+        for u in range(3 * UNITS_PER_BLOCK, FIRST_GPSIMD_UNIT):
+            quantise_unit(u)
+
+        def regroup_on_gpsimd(u):
+            b, g, half = u // UNITS_PER_BLOCK, (u % UNITS_PER_BLOCK) // 2, u % 2
+            grouped = tokens.tile(
+                [P, BANK, PACK], BF16, tag="tok_b", name="grouped%d" % u, align_bytes=64
+            )
+            nc.gpsimd.tensor_scalar(
+                out=grouped[:],
+                in0=block_rows[b][:, g, :, BANK * half : BANK * (half + 1)].rearrange(
+                    "p t n -> p n t"
+                ),
+                scalar1=1.0,
+                scalar2=0.0,
+                op0=ALU.mult,
+                op1=ALU.add,
+            )
+            grouped_units[u] = grouped[:].rearrange("p n t -> p (n t)")
+
+        regroup_on_gpsimd(FIRST_GPSIMD_UNIT)
         g_view = out_1.rearrange("(p m) f -> p m f", p=P)
         units = UNITS_PER_BLOCK * (1 + FF_BLOCKS)
         for b in range(1, 1 + FF_BLOCKS):
-            for m0, count in TOKEN_GROUPS:
-                if b == 1:
-                    quantise_h2(m0, count)
-                for m in range(m0, m0 + count):
-                    step = TOK_TILES * (b - 1) + m
-                    to_quantise = FIRST_UNIT_LEFT + step
-                    to_regroup = to_quantise + 3
-                    hidden = work.tile([P, BLOCK], F32, tag="f32")
-                    for half in range(BLOCK // BANK):
-                        acc = psum.tile([P, BANK], F32, tag="acc", bufs=5)
-                        for g in range(PASSES):
-                            t_first = T * g + P * m
-                            w_first = BLOCK * g + BANK * half
-                            nc.tensor.matmul_mx(
-                                out=acc[:],
-                                lhsT=h2_codes[:, t_first : t_first + P].bitcast(FP8X4),
-                                lhsT_scale=h2_scales[:, t_first : t_first + P],
-                                rhs=block_codes[b][:, w_first : w_first + BANK].bitcast(FP8X4),
-                                rhs_scale=block_scales[b][:, w_first : w_first + BANK],
-                                start=(g == 0),
-                                stop=(g == PASSES - 1),
-                            )
-                        ff_first = BLOCK * (b - 1) + BANK * half
-                        nc.vector.tensor_tensor(
-                            out=hidden[:, BANK * half : BANK * (half + 1)],
-                            in0=acc[:],
-                            in1=bias_fc1[:, ff_first : ff_first + BANK],
-                            op=ALU.add,
+            for m in range(TOK_TILES):
+                step = TOK_TILES * (b - 1) + m
+                hidden = work.tile([P, BLOCK], F32, tag="f32")
+                for half in range(BLOCK // BANK):
+                    acc = psum.tile([P, BANK], F32, tag="acc", bufs=5)
+                    for g in range(PASSES):
+                        t_first = T * g + P * m
+                        w_first = BLOCK * g + BANK * half
+                        nc.tensor.matmul_mx(
+                            out=acc[:],
+                            lhsT=h2_codes[:, t_first : t_first + P].bitcast(FP8X4),
+                            lhsT_scale=h2_scales[:, t_first : t_first + P],
+                            rhs=block_codes[b][:, w_first : w_first + BANK].bitcast(FP8X4),
+                            rhs_scale=block_scales[b][:, w_first : w_first + BANK],
+                            start=(g == 0),
+                            stop=(g == PASSES - 1),
                         )
-                    if to_quantise < units:
-                        quantise_unit(to_quantise)
-                    if to_regroup < units:
-                        if to_regroup % 2 == 0:
-                            regroup_unit(to_regroup, nc.vector.tensor_copy)
-                        else:
-                            regroup_unit(to_regroup, nc.scalar.copy)
-                    nc.scalar.activation(out=hidden[:], in_=hidden[:], func=ACT.Gelu)
-                    nc.sync.dma_start(
-                        out=g_view[:, m, BLOCK * (b - 1) : BLOCK * b], in_=hidden[:]
+                    ff_first = BLOCK * (b - 1) + BANK * half
+                    nc.vector.tensor_tensor(
+                        out=hidden[:, BANK * half : BANK * (half + 1)],
+                        in0=acc[:],
+                        in1=bias_fc1[:, ff_first : ff_first + BANK],
+                        op=ALU.add,
                     )
+                u = FIRST_GPSIMD_UNIT + step // STEPS_PER_GPSIMD_UNIT
+                if step % STEPS_PER_GPSIMD_UNIT == STEPS_PER_GPSIMD_UNIT - 1 and u < units:
+                    quantise_unit(u)
+                    if u + 1 < units:
+                        regroup_on_gpsimd(u + 1)
+                nc.scalar.activation(out=hidden[:], in_=hidden[:], func=ACT.Gelu)
+                nc.sync.dma_start(out=g_view[:, m, BLOCK * (b - 1) : BLOCK * b], in_=hidden[:])

@@ -154,9 +154,9 @@ def tile_nestedtensorblock_pb_kernel(
         quantise_unit(1)
         quantise_unit(2)
         quantise_unit(3)
-        load_ff_block(4)
         bias_fc1 = const.tile([P, FF], BF16)
         nc.sync.dma_start(out=bias_fc1[:], in_=b_fc1.partition_broadcast(P))
+        load_ff_block(4)
 
 
         h_words = h_rows[:].bitcast(F32)

from contextlib import ExitStack

import concourse.mybir as mybir
from concourse.masks import make_identity

F32 = mybir.dt.float32
BF16 = mybir.dt.bfloat16
U32 = mybir.dt.uint32
U8 = mybir.dt.uint8
FP8X4 = mybir.dt.float8_e4m3fn_x4
ACT = mybir.ActivationFunctionType
ALU = mybir.AluOpType

P = 128
PACK = 4
K_PASS = P * PACK
T, D, FF = 768, 1024, 4096
PASSES = D // K_PASS
TOK_TILES = T // P
D_CHUNKS = D // P
BANK = 512
BLOCK = 2 * BANK
FF_BLOCKS = FF // BLOCK
UNITS_PER_BLOCK = PASSES * (BLOCK // BANK)
TOKEN_GROUPS = ((0, 4), (4, 2))
FIRST_GPSIMD_UNIT = 3 * UNITS_PER_BLOCK + 2
STEPS_PER_GPSIMD_UNIT = 3
EPS = 1e-5
FLOPS = 2 * T * D * (D + FF)

B_PROJ, LS1, LN_G, LN_B = 0, D_CHUNKS, 2 * D_CHUNKS, 3 * D_CHUNKS


def tile_nestedtensorblock_pb_kernel(
    tc, h_attn, x, w_proj, b_proj, ls1, ln2_g, ln2_b, w_fc1, b_fc1, out_0, out_1
):
    nc = tc.nc
    with ExitStack() as ctx:
        const = ctx.enter_context(tc.tile_pool(name="const", bufs=1))
        tokens = ctx.enter_context(tc.tile_pool(name="tokens", bufs=1))
        weights = ctx.enter_context(tc.tile_pool(name="weights", bufs=4))
        stage = ctx.enter_context(tc.tile_pool(name="stage", bufs=4))
        work = ctx.enter_context(tc.tile_pool(name="work", bufs=8))
        psum = ctx.enter_context(tc.psum_pool(name="psum", bufs=1))

        vec_rows = const.tile([P, P], BF16)
        nc.vector.memset(vec_rows[:], 0.0)
        for first_row, vec in ((B_PROJ, b_proj), (LS1, ls1), (LN_G, ln2_g), (LN_B, ln2_b)):
            nc.scalar.dma_start(
                out=vec_rows[first_row : first_row + D_CHUNKS, :],
                in_=vec.rearrange("(r c) -> r c", c=P),
            )

        block_rows = {}
        block_codes = {}
        block_scales = {}

        def new_block_rows(b):
            block_rows[b] = weights.tile(
                [P, PASSES, PACK, BLOCK], BF16, tag="w_rows", name="w_rows%d" % b
            )

        def new_block_codes(b):
            block_codes[b] = weights.tile(
                [P, PASSES * BLOCK], U32, tag="w_codes", name="w_codes%d" % b, align_bytes=64
            )
            block_scales[b] = weights.tile(
                [P, PASSES * BLOCK], U8, tag="w_scales", name="w_scales%d" % b, align_bytes=64
            )

        new_block_rows(0)
        wp_view = w_proj.rearrange("(g u q e) n -> q g u e n", g=PASSES, u=2, e=2)
        for g in range(PASSES):
            for u in range(2):
                nc.sync.dma_start(
                    out=block_rows[0][:, g, 2 * u : 2 * u + 2, :], in_=wp_view[:, g, u, :, :]
                )

        h_rows = tokens.tile([P, TOK_TILES * D], BF16, tag="tok_a")
        h_view = h_attn.rearrange("(p m) d -> p m d", p=P)
        for pair in range(TOK_TILES // 2):
            nc.sync.dma_start(
                out=h_rows[:, 2 * D * pair : 2 * D * (pair + 1)].rearrange("p (m d) -> p m d", m=2),
                in_=h_view[:, 2 * pair : 2 * pair + 2, :],
            )

        wf_view = w_fc1.rearrange("(g t p) n -> p g t n", g=PASSES, t=PACK)

        def load_ff_block(b):
            new_block_rows(b)
            for g in range(PASSES):
                nc.sync.dma_start(
                    out=block_rows[b][:, g, :, :],
                    in_=wf_view[:, g, :, BLOCK * (b - 1) : BLOCK * b],
                )

        load_ff_block(1)
        x_rows = const.tile([P, TOK_TILES, D], BF16)
        nc.sync.dma_start(out=x_rows[:], in_=x.rearrange("(p m) d -> p m d", p=P))
        load_ff_block(2)
        load_ff_block(3)

        ident_f32 = const.tile([P, P], F32)
        make_identity(nc, ident_f32[:])
        ident_bf16 = const.tile([P, P], BF16)
        nc.vector.tensor_copy(out=ident_bf16[:], in_=ident_f32[:])
        neg_half = const.tile([P, 1], F32)
        nc.vector.memset(neg_half[:], -0.5)
        first_gelu = const.tile([P, 1], F32)
        nc.scalar.activation(out=first_gelu[:], in_=neg_half[:], func=ACT.Gelu)

        vec_cols = const.tile([P, 4 * D_CHUNKS], F32)
        ls1_b = const.tile([P, D_CHUNKS], F32)

        def transpose_vectors():
            vec_ps = psum.tile([P, P], BF16, tag="turn", bufs=3)
            nc.tensor.transpose(vec_ps[:], vec_rows[:], ident_bf16[:])
            nc.vector.tensor_copy(out=vec_cols[:], in_=vec_ps[:, 0 : 4 * D_CHUNKS])
            nc.vector.tensor_mul(
                ls1_b[:], vec_cols[:, LS1 : LS1 + D_CHUNKS], vec_cols[:, B_PROJ : B_PROJ + D_CHUNKS]
            )

        for b in range(4):
            new_block_codes(b)
        grouped_units = {}

        def regroup_unit(u, copy):
            b, g, half = u // UNITS_PER_BLOCK, (u % UNITS_PER_BLOCK) // 2, u % 2
            grouped = stage.tile(
                [P, BANK * PACK], BF16, tag="grouped", name="grouped%d" % u, align_bytes=64
            )
            copy(
                out=grouped[:].rearrange("p (c i t) -> p c t i", i=4, t=PACK),
                in_=block_rows[b][:, g, :, BANK * half : BANK * (half + 1)].rearrange(
                    "p t (c i) -> p c t i", i=4
                ),
            )
            grouped_units[u] = grouped[:]

        def quantise_unit(u):
            b, g, half = u // UNITS_PER_BLOCK, (u % UNITS_PER_BLOCK) // 2, u % 2
            first = BLOCK * g + BANK * half
            nc.vector.quantize_mx(
                out=block_codes[b][:, first : first + BANK].bitcast(FP8X4),
                scales=block_scales[b][:, first : first + BANK],
                in_=grouped_units[u],
            )

        regroup_unit(0, nc.vector.tensor_copy)
        regroup_unit(1, nc.scalar.copy)
        quantise_unit(0)
        regroup_unit(2, nc.vector.tensor_copy)
        regroup_unit(3, nc.scalar.copy)
        quantise_unit(1)
        quantise_unit(2)
        quantise_unit(3)
        bias_fc1 = const.tile([P, FF], BF16)
        nc.sync.dma_start(out=bias_fc1[:], in_=b_fc1.partition_broadcast(P))
        load_ff_block(4)


        h_words = h_rows[:].bitcast(F32)
        h_grouped = tokens.tile([P, PASSES * T * PACK], BF16, tag="tok_b", align_bytes=64)
        h_grouped_words = h_grouped[:].bitcast(F32).rearrange(
            "p (g r u) -> p g r u", g=PASSES, u=2
        )
        h_codes = tokens.tile([P, PASSES * T], U32, tag="tok_codes", align_bytes=64)
        h_scales = tokens.tile([P, PASSES * T], U8, tag="tok_scales", align_bytes=64)
        for pair in range(TOK_TILES // 2):
            for m in (2 * pair, 2 * pair + 1):
                turned = psum.tile([P, PASSES, 2, P], F32, tag="turn", bufs=3)
                for g in range(PASSES):
                    for u in range(2):
                        first_word = (D // 2) * m + (K_PASS // 2) * g + P * u
                        nc.tensor.transpose(
                            turned[:, g, u, :],
                            h_words[:, first_word : first_word + P],
                            ident_f32[:],
                        )
                nc.scalar.copy(
                    out=h_grouped_words[:, :, P * m : P * (m + 1), :],
                    in_=turned[:].rearrange("p g u r -> p g r u"),
                )
            for g in range(PASSES):
                first = T * g + 2 * P * pair
                nc.vector.quantize_mx(
                    out=h_codes[:, first : first + 2 * P].bitcast(FP8X4),
                    scales=h_scales[:, first : first + 2 * P],
                    in_=h_grouped[:, PACK * first : PACK * (first + 2 * P)],
                )
            if pair == 0:
                transpose_vectors()

        branch_t = [
            tokens.tile([P, 4, T], F32, tag="tok_a", name="branch_t0"),
            tokens.tile([P, 4, T], F32, tag="tok_b", name="branch_t1", align_bytes=64),
        ]
        for m0, count in TOKEN_GROUPS:
            for c in range(D_CHUNKS):
                acc = psum.tile([P, BANK], F32, tag="acc", bufs=5)
                for g in range(PASSES):
                    w_first = BLOCK * g + P * c
                    t_first = T * g + P * m0
                    nc.tensor.matmul_mx(
                        out=acc[:, 0 : P * count],
                        lhsT=block_codes[0][:, w_first : w_first + P].bitcast(FP8X4),
                        lhsT_scale=block_scales[0][:, w_first : w_first + P],
                        rhs=h_codes[:, t_first : t_first + P * count].bitcast(FP8X4),
                        rhs_scale=h_scales[:, t_first : t_first + P * count],
                        start=(g == 0),
                        stop=(g == PASSES - 1),
                    )
                nc.scalar.activation(
                    out=branch_t[c // 4][:, c % 4, P * m0 : P * (m0 + count)],
                    in_=acc[:, 0 : P * count],
                    func=ACT.Identity,
                    scale=vec_cols[:, LS1 + c : LS1 + c + 1],
                    bias=ls1_b[:, c : c + 1],
                )
        new_block_codes(4)
        regroup_unit(4, nc.vector.tensor_copy)
        regroup_unit(5, nc.vector.tensor_copy)
        quantise_unit(4)
        regroup_unit(6, nc.vector.tensor_copy)
        quantise_unit(5)
        regroup_unit(7, nc.vector.tensor_copy)
        quantise_unit(6)
        quantise_unit(7)

        x_mid = const.tile([P, TOK_TILES, D], F32)
        half_sums = const.tile([P, TOK_TILES, 2], F32)
        neg_mean = const.tile([P, TOK_TILES], F32)
        sum_sq = const.tile([P, TOK_TILES], F32)
        var_eps = const.tile([P, TOK_TILES], F32)
        rstd = const.tile([P, TOK_TILES], F32)
        x_mid_view = out_0.rearrange("(p m) d -> p m d", p=P)
        x_hat = []
        for m in range(TOK_TILES):
            for half in range(2):
                branch = psum.tile([P, BANK], F32, tag="turn", bufs=3)
                for q in range(4):
                    nc.tensor.transpose(
                        branch[:, P * q : P * (q + 1)],
                        branch_t[half][:, q, P * m : P * (m + 1)],
                        ident_f32[:],
                    )
                nc.vector.scalar_tensor_tensor(
                    out=x_mid[:, m, BANK * half : BANK * (half + 1)],
                    in0=branch[:],
                    scalar=1.0,
                    in1=x_rows[:, m, BANK * half : BANK * (half + 1)],
                    op0=ALU.mult,
                    op1=ALU.add,
                    accum_out=half_sums[:, m, half : half + 1],
                )
            nc.sync.dma_start(out=x_mid_view[:, m, :], in_=x_mid[:, m, :])
            nc.vector.tensor_scalar(
                out=neg_mean[:, m : m + 1],
                in0=half_sums[:, m, 0:1],
                scalar1=half_sums[:, m, 1:2],
                scalar2=-1.0 / D,
                op0=ALU.add,
                op1=ALU.mult,
            )
            normed = work.tile([P, D], F32, tag="f32", name="x_hat%d" % m)
            nc.scalar.activation(
                out=normed[:],
                in_=x_mid[:, m, :],
                func=ACT.Square,
                bias=neg_mean[:, m : m + 1],
                scale=1.0,
                accum_out=sum_sq[:, m : m + 1],
            )
            nc.vector.tensor_scalar(
                out=var_eps[:, m : m + 1],
                in0=sum_sq[:, m : m + 1],
                scalar1=1.0 / D,
                scalar2=EPS,
                op0=ALU.mult,
                op1=ALU.add,
            )
            nc.gpsimd.tensor_tensor(
                out=rstd[:, m : m + 1], in0=var_eps[:, m : m + 1], in1=neg_half[:], op=ALU.pow
            )
            nc.vector.tensor_scalar(
                out=normed[:],
                in0=x_mid[:, m, :],
                scalar1=neg_mean[:, m : m + 1],
                scalar2=rstd[:, m : m + 1],
                op0=ALU.add,
                op1=ALU.mult,
            )
            x_hat.append(normed)

        h2_planes = tokens.tile([P, D_CHUNKS * T], BF16, tag="tok_a")
        h2_grouped = tokens.tile([P, PASSES * T * PACK], BF16, tag="tok_b", align_bytes=64)
        h2_codes = tokens.tile([P, PASSES * T], U32, tag="tok_codes", align_bytes=64)
        h2_scales = tokens.tile([P, PASSES * T], U8, tag="tok_scales", align_bytes=64)
        h2_chunks = h2_planes[:].rearrange("p (c r) -> p c r", c=D_CHUNKS)
        for m0, count in TOKEN_GROUPS:
            for c in range(D_CHUNKS):
                turned = psum.tile([P, BANK], F32, tag="turn", bufs=3)
                for i in range(count):
                    nc.tensor.transpose(
                        turned[:, P * i : P * (i + 1)],
                        x_hat[m0 + i][:, P * c : P * (c + 1)],
                        ident_f32[:],
                    )
                nc.scalar.activation(
                    out=h2_chunks[:, c, P * m0 : P * (m0 + count)],
                    in_=turned[:, 0 : P * count],
                    func=ACT.Identity,
                    scale=vec_cols[:, LN_G + c : LN_G + c + 1],
                    bias=vec_cols[:, LN_B + c : LN_B + c + 1],
                )
            for g in range(PASSES):
                first = T * g + P * m0
                nc.vector.tensor_copy(
                    out=h2_grouped[:, PACK * first : PACK * (first + P * count)].rearrange(
                        "p (c i t) -> p c t i", i=4, t=PACK
                    ),
                    in_=h2_chunks[:, PACK * g : PACK * (g + 1), P * m0 : P * (m0 + count)].rearrange(
                        "p t (c i) -> p c t i", i=4
                    ),
                )
            for g in range(PASSES):
                first = T * g + P * m0
                nc.vector.quantize_mx(
                    out=h2_codes[:, first : first + P * count].bitcast(FP8X4),
                    scales=h2_scales[:, first : first + P * count],
                    in_=h2_grouped[:, PACK * first : PACK * (first + P * count)],
                )

        for u in range(2 * UNITS_PER_BLOCK, 3 * UNITS_PER_BLOCK):
            regroup_unit(u, nc.scalar.copy)
        for u in range(2 * UNITS_PER_BLOCK, 3 * UNITS_PER_BLOCK):
            quantise_unit(u)
        for u in range(3 * UNITS_PER_BLOCK, FIRST_GPSIMD_UNIT):
            regroup_unit(u, nc.vector.tensor_copy)
        for u in range(3 * UNITS_PER_BLOCK, FIRST_GPSIMD_UNIT):
            quantise_unit(u)

        def regroup_on_gpsimd(u):
            b, g, half = u // UNITS_PER_BLOCK, (u % UNITS_PER_BLOCK) // 2, u % 2
            grouped = tokens.tile(
                [P, BANK, PACK], BF16, tag="tok_b", name="grouped%d" % u, align_bytes=64
            )
            nc.gpsimd.tensor_scalar(
                out=grouped[:],
                in0=block_rows[b][:, g, :, BANK * half : BANK * (half + 1)].rearrange(
                    "p t n -> p n t"
                ),
                scalar1=1.0,
                scalar2=0.0,
                op0=ALU.mult,
                op1=ALU.add,
            )
            grouped_units[u] = grouped[:].rearrange("p n t -> p (n t)")

        regroup_on_gpsimd(FIRST_GPSIMD_UNIT)
        g_view = out_1.rearrange("(p m) f -> p m f", p=P)
        units = UNITS_PER_BLOCK * (1 + FF_BLOCKS)
        for b in range(1, 1 + FF_BLOCKS):
            for m in range(TOK_TILES):
                step = TOK_TILES * (b - 1) + m
                hidden = work.tile([P, BLOCK], F32, tag="f32")
                for half in range(BLOCK // BANK):
                    acc = psum.tile([P, BANK], F32, tag="acc", bufs=5)
                    for g in range(PASSES):
                        t_first = T * g + P * m
                        w_first = BLOCK * g + BANK * half
                        nc.tensor.matmul_mx(
                            out=acc[:],
                            lhsT=h2_codes[:, t_first : t_first + P].bitcast(FP8X4),
                            lhsT_scale=h2_scales[:, t_first : t_first + P],
                            rhs=block_codes[b][:, w_first : w_first + BANK].bitcast(FP8X4),
                            rhs_scale=block_scales[b][:, w_first : w_first + BANK],
                            start=(g == 0),
                            stop=(g == PASSES - 1),
                        )
                    ff_first = BLOCK * (b - 1) + BANK * half
                    nc.vector.tensor_tensor(
                        out=hidden[:, BANK * half : BANK * (half + 1)],
                        in0=acc[:],
                        in1=bias_fc1[:, ff_first : ff_first + BANK],
                        op=ALU.add,
                    )
                u = FIRST_GPSIMD_UNIT + step // STEPS_PER_GPSIMD_UNIT
                if step % STEPS_PER_GPSIMD_UNIT == STEPS_PER_GPSIMD_UNIT - 1 and u < units:
                    quantise_unit(u)
                    if u + 1 < units:
                        regroup_on_gpsimd(u + 1)
                nc.scalar.activation(out=hidden[:], in_=hidden[:], func=ACT.Gelu)
                nc.sync.dma_start(out=g_view[:, m, BLOCK * (b - 1) : BLOCK * b], in_=hidden[:])
